import numpy as np
import ml_dtypes

BF16 = ml_dtypes.bfloat16


def bf(x):
    return np.asarray(x, np.float32).astype(BF16)


def f32(x):
    return np.asarray(x, np.float32)


def f64(x):
    return np.asarray(x).astype(np.float64)


def striped(idx):
    return np.tile(idx.reshape(-1, 16).T, (8, 1))


C, S, N = 384, 512, 256


def setup_inputs():
    return {"t": f32(np.random.standard_normal((C, S))), "z_noise": f32(np.random.standard_normal((C, N))), "log_s_c": f32(0.3 * np.random.standard_normal((C, N))), "offs": striped(np.random.permutation(S)[:N])}


def reference(t, z_noise, log_s_c, offs):
    idx = offs[:16].T.reshape(-1)
    return (f64(t)[:, idx] + f64(z_noise)) * np.exp(f64(log_s_c))

@@ -1,0 +1,43 @@
+import concourse.mybir as mybir
+
+F32 = mybir.dt.float32
+U16 = mybir.dt.uint16
+ADD = mybir.AluOpType.add
+MULT = mybir.AluOpType.mult
+EXP = mybir.ActivationFunctionType.Exp
+
+P = 128
+
+
+def tile_linearcategoricalencoding_kernel(tc, t, z_noise, log_s_c, offs, out):
+    nc = tc.nc
+    channels, categories = t.shape
+    tokens = z_noise.shape[1]
+    blocks = channels // P
+
+    with (
+        tc.tile_pool(name="held", bufs=1) as held,
+        tc.tile_pool(name="work", bufs=blocks) as work,
+    ):
+        offsets = held.tile([P, tokens // 16], U16, name="offsets")
+        nc.sync.dma_start(offsets[:], offs)
+
+        for b in range(blocks):
+            rows = slice(b * P, (b + 1) * P)
+
+            table = work.tile([P, categories], F32)
+            nc.sync.dma_start(table[:], t[rows, :])
+            noise = work.tile([P, tokens], F32)
+            nc.sync.dma_start(noise[:], z_noise[rows, :])
+            log_scale = work.tile([P, tokens], F32)
+            nc.sync.dma_start(log_scale[:], log_s_c[rows, :])
+
+            scale = work.tile([P, tokens], F32)
+            nc.scalar.activation(scale[:], log_scale[:], EXP)
+
+            shifted = work.tile([P, tokens], F32)
+            nc.vector.tensor_tensor(shifted[:], table[:].indirect(offsets[:]), noise[:], ADD)
+
+            encoded = work.tile([P, tokens], F32)
+            nc.vector.tensor_tensor(encoded[:], shifted[:], scale[:], MULT)
+            nc.sync.dma_start(out[rows, :], encoded[:])

@@ -15,29 +15,28 @@ def tile_linearcategoricalencoding_kernel(tc, t, z_noise, log_s_c, offs, out):
     tokens = z_noise.shape[1]
     blocks = channels // P
 
-    with (
-        tc.tile_pool(name="held", bufs=1) as held,
-        tc.tile_pool(name="work", bufs=blocks) as work,
-    ):
+    t_blocks = t.rearrange("(p b) s -> p b s", b=blocks)
+    out_blocks = out.rearrange("(p b) n -> p b n", b=blocks)
+
+    with tc.tile_pool(name="held", bufs=1) as held:
         offsets = held.tile([P, tokens // 16], U16, name="offsets")
         nc.sync.dma_start(offsets[:], offs)
 
+        tables = [held.tile([P, categories], F32, name=f"table{b}") for b in range(blocks)]
+        noise = held.tile([P, blocks * tokens], F32, name="noise")
+        log_scale = held.tile([P, blocks * tokens], F32, name="log_scale")
+        nc.sync.dma_start(tables[0][:], t_blocks[:, 0, :])
+        nc.sync.dma_start(noise[:], z_noise.rearrange("(p b) n -> p (b n)", b=blocks))
+        nc.sync.dma_start(log_scale[:], log_s_c.rearrange("(p b) n -> p (b n)", b=blocks))
+        for b in range(1, blocks):
+            nc.sync.dma_start(tables[b][:], t_blocks[:, b, :])
+
+        scale = held.tile([P, blocks * tokens], F32, name="scale")
+        shifted = held.tile([P, blocks * tokens], F32, name="shifted")
+        encoded = held.tile([P, blocks * tokens], F32, name="encoded")
         for b in range(blocks):
-            rows = slice(b * P, (b + 1) * P)
-
-            table = work.tile([P, categories], F32)
-            nc.sync.dma_start(table[:], t[rows, :])
-            noise = work.tile([P, tokens], F32)
-            nc.sync.dma_start(noise[:], z_noise[rows, :])
-            log_scale = work.tile([P, tokens], F32)
-            nc.sync.dma_start(log_scale[:], log_s_c[rows, :])
-
-            scale = work.tile([P, tokens], F32)
-            nc.scalar.activation(scale[:], log_scale[:], EXP)
-
-            shifted = work.tile([P, tokens], F32)
-            nc.vector.tensor_tensor(shifted[:], table[:].indirect(offsets[:]), noise[:], ADD)
-
-            encoded = work.tile([P, tokens], F32)
-            nc.vector.tensor_tensor(encoded[:], shifted[:], scale[:], MULT)
-            nc.sync.dma_start(out[rows, :], encoded[:])
+            cols = slice(b * tokens, (b + 1) * tokens)
+            nc.scalar.activation(scale[:, cols], log_scale[:, cols], EXP)
+            nc.vector.tensor_tensor(shifted[:, cols], tables[b][:].indirect(offsets[:]), noise[:, cols], ADD)
+            nc.vector.tensor_tensor(encoded[:, cols], shifted[:, cols], scale[:, cols], MULT)
+            nc.sync.dma_start(out_blocks[:, b, :], encoded[:, cols])

@@ -15,28 +15,26 @@ def tile_linearcategoricalencoding_kernel(tc, t, z_noise, log_s_c, offs, out):
     tokens = z_noise.shape[1]
     blocks = channels // P
 
-    t_blocks = t.rearrange("(p b) s -> p b s", b=blocks)
-    out_blocks = out.rearrange("(p b) n -> p b n", b=blocks)
-
     with tc.tile_pool(name="held", bufs=1) as held:
         offsets = held.tile([P, tokens // 16], U16, name="offsets")
         nc.sync.dma_start(offsets[:], offs)
 
         tables = [held.tile([P, categories], F32, name=f"table{b}") for b in range(blocks)]
-        noise = held.tile([P, blocks * tokens], F32, name="noise")
-        log_scale = held.tile([P, blocks * tokens], F32, name="log_scale")
-        nc.sync.dma_start(tables[0][:], t_blocks[:, 0, :])
-        nc.sync.dma_start(noise[:], z_noise.rearrange("(p b) n -> p (b n)", b=blocks))
-        nc.sync.dma_start(log_scale[:], log_s_c.rearrange("(p b) n -> p (b n)", b=blocks))
-        for b in range(1, blocks):
-            nc.sync.dma_start(tables[b][:], t_blocks[:, b, :])
-
-        scale = held.tile([P, blocks * tokens], F32, name="scale")
-        shifted = held.tile([P, blocks * tokens], F32, name="shifted")
-        encoded = held.tile([P, blocks * tokens], F32, name="encoded")
+        noises = [held.tile([P, tokens], F32, name=f"noise{b}") for b in range(blocks)]
+        log_scales = [held.tile([P, tokens], F32, name=f"log_scale{b}") for b in range(blocks)]
         for b in range(blocks):
-            cols = slice(b * tokens, (b + 1) * tokens)
-            nc.scalar.activation(scale[:, cols], log_scale[:, cols], EXP)
-            nc.vector.tensor_tensor(shifted[:, cols], tables[b][:].indirect(offsets[:]), noise[:, cols], ADD)
-            nc.vector.tensor_tensor(encoded[:, cols], shifted[:, cols], scale[:, cols], MULT)
-            nc.sync.dma_start(out_blocks[:, b, :], encoded[:, cols])
+            nc.sync.dma_start(tables[b][:], t[b * P : (b + 1) * P, :])
+            nc.sync.dma_start(noises[b][:], z_noise[b * P : (b + 1) * P, :])
+        for b in range(blocks):
+            nc.sync.dma_start(log_scales[b][:], log_s_c[b * P : (b + 1) * P, :])
+
+        for b in range(blocks):
+            shifted = held.tile([P, tokens], F32, name=f"shifted{b}")
+            nc.vector.tensor_tensor(shifted[:], tables[b][:].indirect(offsets[:]), noises[b][:], ADD)
+
+            scale = held.tile([P, tokens], F32, name=f"scale{b}")
+            nc.scalar.activation(scale[:], log_scales[b][:], EXP)
+
+            encoded = held.tile([P, tokens], F32, name=f"encoded{b}")
+            nc.vector.tensor_tensor(encoded[:], shifted[:], scale[:], MULT)
+            nc.sync.dma_start(out[b * P : (b + 1) * P, :], encoded[:])

@@ -22,11 +22,16 @@ def tile_linearcategoricalencoding_kernel(tc, t, z_noise, log_s_c, offs, out):
         tables = [held.tile([P, categories], F32, name=f"table{b}") for b in range(blocks)]
         noises = [held.tile([P, tokens], F32, name=f"noise{b}") for b in range(blocks)]
         log_scales = [held.tile([P, tokens], F32, name=f"log_scale{b}") for b in range(blocks)]
+
+        loads = []
         for b in range(blocks):
-            nc.sync.dma_start(tables[b][:], t[b * P : (b + 1) * P, :])
-            nc.sync.dma_start(noises[b][:], z_noise[b * P : (b + 1) * P, :])
+            loads.append((tables[b], t[b * P : (b + 1) * P, :]))
+            loads.append((noises[b], z_noise[b * P : (b + 1) * P, :]))
         for b in range(blocks):
-            nc.sync.dma_start(log_scales[b][:], log_s_c[b * P : (b + 1) * P, :])
+            loads.append((log_scales[b], log_s_c[b * P : (b + 1) * P, :]))
+        for i, (tile, source) in enumerate(loads):
+            queue = nc.sync if i % 2 == 0 else nc.scalar
+            queue.dma_start(tile[:], source)
 
         for b in range(blocks):
             shifted = held.tile([P, tokens], F32, name=f"shifted{b}")

@@ -19,23 +19,19 @@ def tile_linearcategoricalencoding_kernel(tc, t, z_noise, log_s_c, offs, out):
         offsets = held.tile([P, tokens // 16], U16, name="offsets")
         nc.sync.dma_start(offsets[:], offs)
 
-        tables = [held.tile([P, categories], F32, name=f"table{b}") for b in range(blocks)]
-        noises = [held.tile([P, tokens], F32, name=f"noise{b}") for b in range(blocks)]
-        log_scales = [held.tile([P, tokens], F32, name=f"log_scale{b}") for b in range(blocks)]
+        noise = held.tile([P, blocks, tokens], F32, name="noise")
+        nc.scalar.dma_start(noise[:], z_noise.rearrange("(b p) n -> p b n", p=P))
 
-        loads = []
+        tables = [held.tile([P, categories], F32, name=f"table{b}") for b in range(blocks)]
+        log_scales = [held.tile([P, tokens], F32, name=f"log_scale{b}") for b in range(blocks)]
         for b in range(blocks):
-            loads.append((tables[b], t[b * P : (b + 1) * P, :]))
-            loads.append((noises[b], z_noise[b * P : (b + 1) * P, :]))
+            nc.sync.dma_start(tables[b][:], t[b * P : (b + 1) * P, :])
         for b in range(blocks):
-            loads.append((log_scales[b], log_s_c[b * P : (b + 1) * P, :]))
-        for i, (tile, source) in enumerate(loads):
-            queue = nc.sync if i % 2 == 0 else nc.scalar
-            queue.dma_start(tile[:], source)
+            nc.sync.dma_start(log_scales[b][:], log_s_c[b * P : (b + 1) * P, :])
 
         for b in range(blocks):
             shifted = held.tile([P, tokens], F32, name=f"shifted{b}")
-            nc.vector.tensor_tensor(shifted[:], tables[b][:].indirect(offsets[:]), noises[b][:], ADD)
+            nc.vector.tensor_tensor(shifted[:], tables[b][:].indirect(offsets[:]), noise[:, b, :], ADD)
 
             scale = held.tile([P, tokens], F32, name=f"scale{b}")
             nc.scalar.activation(scale[:], log_scales[b][:], EXP)

@@ -17,7 +17,6 @@ def tile_linearcategoricalencoding_kernel(tc, t, z_noise, log_s_c, offs, out):
 
     with tc.tile_pool(name="held", bufs=1) as held:
         offsets = held.tile([P, tokens // 16], U16, name="offsets")
-        nc.sync.dma_start(offsets[:], offs)
 
         noise = held.tile([P, blocks, tokens], F32, name="noise")
         nc.scalar.dma_start(noise[:], z_noise.rearrange("(b p) n -> p b n", p=P))
@@ -26,6 +25,8 @@ def tile_linearcategoricalencoding_kernel(tc, t, z_noise, log_s_c, offs, out):
         log_scales = [held.tile([P, tokens], F32, name=f"log_scale{b}") for b in range(blocks)]
         for b in range(blocks):
             nc.sync.dma_start(tables[b][:], t[b * P : (b + 1) * P, :])
+            if b == 0:
+                nc.sync.dma_start(offsets[:], offs)
         for b in range(blocks):
             nc.sync.dma_start(log_scales[b][:], log_s_c[b * P : (b + 1) * P, :])
 

@@ -15,20 +15,24 @@ def tile_linearcategoricalencoding_kernel(tc, t, z_noise, log_s_c, offs, out):
     tokens = z_noise.shape[1]
     blocks = channels // P
 
+    t_blocks = t.rearrange("(p b) s -> p b s", b=blocks)
+    log_s_c_blocks = log_s_c.rearrange("(p b) n -> p b n", b=blocks)
+    out_blocks = out.rearrange("(p b) n -> p b n", b=blocks)
+
     with tc.tile_pool(name="held", bufs=1) as held:
         offsets = held.tile([P, tokens // 16], U16, name="offsets")
 
         noise = held.tile([P, blocks, tokens], F32, name="noise")
-        nc.scalar.dma_start(noise[:], z_noise.rearrange("(b p) n -> p b n", p=P))
+        nc.scalar.dma_start(noise[:], z_noise.rearrange("(p b) n -> p b n", b=blocks))
 
         tables = [held.tile([P, categories], F32, name=f"table{b}") for b in range(blocks)]
         log_scales = [held.tile([P, tokens], F32, name=f"log_scale{b}") for b in range(blocks)]
         for b in range(blocks):
-            nc.sync.dma_start(tables[b][:], t[b * P : (b + 1) * P, :])
+            nc.sync.dma_start(tables[b][:], t_blocks[:, b, :])
             if b == 0:
                 nc.sync.dma_start(offsets[:], offs)
         for b in range(blocks):
-            nc.sync.dma_start(log_scales[b][:], log_s_c[b * P : (b + 1) * P, :])
+            nc.sync.dma_start(log_scales[b][:], log_s_c_blocks[:, b, :])
 
         for b in range(blocks):
             shifted = held.tile([P, tokens], F32, name=f"shifted{b}")
@@ -39,4 +43,4 @@ def tile_linearcategoricalencoding_kernel(tc, t, z_noise, log_s_c, offs, out):
 
             encoded = held.tile([P, tokens], F32, name=f"encoded{b}")
             nc.vector.tensor_tensor(encoded[:], shifted[:], scale[:], MULT)
-            nc.sync.dma_start(out[b * P : (b + 1) * P, :], encoded[:])
+            nc.sync.dma_start(out_blocks[:, b, :], encoded[:])

import concourse.mybir as mybir

F32 = mybir.dt.float32
U16 = mybir.dt.uint16
ADD = mybir.AluOpType.add
MULT = mybir.AluOpType.mult
EXP = mybir.ActivationFunctionType.Exp

P = 128


def tile_linearcategoricalencoding_kernel(tc, t, z_noise, log_s_c, offs, out):
    nc = tc.nc
    channels, categories = t.shape
    tokens = z_noise.shape[1]
    blocks = channels // P

    t_blocks = t.rearrange("(p b) s -> p b s", b=blocks)
    log_s_c_blocks = log_s_c.rearrange("(p b) n -> p b n", b=blocks)
    out_blocks = out.rearrange("(p b) n -> p b n", b=blocks)

    with tc.tile_pool(name="held", bufs=1) as held:
        offsets = held.tile([P, tokens // 16], U16, name="offsets")

        noise = held.tile([P, blocks, tokens], F32, name="noise")
        nc.scalar.dma_start(noise[:], z_noise.rearrange("(p b) n -> p b n", b=blocks))

        tables = [held.tile([P, categories], F32, name=f"table{b}") for b in range(blocks)]
        log_scales = [held.tile([P, tokens], F32, name=f"log_scale{b}") for b in range(blocks)]
        for b in range(blocks):
            nc.sync.dma_start(tables[b][:], t_blocks[:, b, :])
            if b == 0:
                nc.sync.dma_start(offsets[:], offs)
        for b in range(blocks):
            nc.sync.dma_start(log_scales[b][:], log_s_c_blocks[:, b, :])

        for b in range(blocks):
            shifted = held.tile([P, tokens], F32, name=f"shifted{b}")
            nc.vector.tensor_tensor(shifted[:], tables[b][:].indirect(offsets[:]), noise[:, b, :], ADD)

            scale = held.tile([P, tokens], F32, name=f"scale{b}")
            nc.scalar.activation(scale[:], log_scales[b][:], EXP)

            encoded = held.tile([P, tokens], F32, name=f"encoded{b}")
            nc.vector.tensor_tensor(encoded[:], shifted[:], scale[:], MULT)
            nc.sync.dma_start(out_blocks[:, b, :], encoded[:])
